import numpy as np
import ml_dtypes

BF16 = ml_dtypes.bfloat16


def bf(x):
    return np.asarray(x, np.float32).astype(BF16)


def f32(x):
    return np.asarray(x, np.float32)


def f64(x):
    return np.asarray(x).astype(np.float64)


def striped(idx):
    return np.tile(idx.reshape(-1, 16).T, (8, 1))


B, D, S, K, H, N, K2 = 512, 2048, 2048, 8, 1024, 8192, 10


def setup_inputs():
    idx = np.concatenate([np.random.permutation(S)[:H] for _ in range(K)])
    return {"xt": f32(np.random.standard_normal((D, B))), "center": f32(np.random.standard_normal((D, 1))), "rotation": f32(np.random.standard_normal((D, S)) / np.sqrt(D)), "w1": f32(np.random.standard_normal((1, N)) / np.sqrt(H)), "b1": f32(np.random.uniform(0.2, 1.0, (1, K))), "w2": f32(np.random.uniform(0.2, 0.5, (1, K2))), "b2": f32(np.random.uniform(0.3, 0.8, (1, 1))), "female": f32(np.random.standard_normal((B, 1))), "age": f32(np.random.standard_normal((B, 1))), "offs": striped(idx)}


def reference(xt, center, rotation, w1, b1, w2, b2, female, age, offs):
    idx = offs[:16].T.reshape(-1)
    p = (f64(xt) - f64(center)).T @ f64(rotation)
    t = p[:, idx] * f64(w1)
    u = t.reshape(B, K, H).sum(axis=2) + f64(b1)
    v = f64(w2)
    return (u * v[:, :K]).sum(axis=1, keepdims=True) + v[0, K] * f64(age) + v[0, K + 1] * f64(female) + f64(b2)

@@ -1,0 +1,148 @@
+import concourse.mybir as mybir
+from concourse.masks import make_identity
+
+F32 = mybir.dt.float32
+BF16 = mybir.dt.bfloat16
+U16 = mybir.dt.uint16
+ADD = mybir.AluOpType.add
+MULT = mybir.AluOpType.mult
+COPY = mybir.ActivationFunctionType.Copy
+IDENTITY = mybir.ActivationFunctionType.Identity
+
+P = 128
+B, D, S = 512, 2048, 2048
+K, H = 8, 1024
+N = K * H
+D_TILES = D // P
+BLOCKS = B // P
+BANK = 512
+BANKS = S // BANK
+XT_COLS = 2 * P
+XT_TILES = S // XT_COLS
+W1_COLS = S
+RING_SLOTS = N // W1_COLS + D_TILES // XT_TILES
+
+FLOPS = 2 * B * D * S + 2 * B * N
+
+
+def tile_pcgrimage_b_kernel(tc, xt, center, rotation, w1, b1, w2, b2, female, age, offs, out):
+    nc = tc.nc
+    xt_rows = xt.rearrange("(p t) b -> p t b", t=D_TILES)
+    rotation_rows = rotation.rearrange("(p t) s -> p t s", t=D_TILES)
+
+    with (
+        tc.tile_pool(name="held", bufs=1) as held,
+        tc.tile_pool(name="ring", bufs=RING_SLOTS) as ring,
+        tc.tile_pool(name="products", bufs=3) as products,
+        tc.psum_pool(name="banks", bufs=8) as banks,
+    ):
+        offsets = held.tile([P, N // 16], U16, name="offsets")
+        nc.sync.dma_start(offsets[:], offs)
+
+        center_cols = held.tile([P, D_TILES], F32, name="center_cols")
+        nc.scalar.dma_start(center_cols[:], center.rearrange("(p t) one -> p (t one)", t=D_TILES))
+        b1_rows = held.tile([P, K], F32, name="b1_rows")
+        nc.scalar.dma_start(b1_rows[:], b1[0, :].partition_broadcast(P))
+        w2_rows = held.tile([P, K + 2], F32, name="w2_rows")
+        nc.scalar.dma_start(w2_rows[:], w2[0, :].partition_broadcast(P))
+        b2_rows = held.tile([P, 1], F32, name="b2_rows")
+        nc.scalar.dma_start(b2_rows[:], b2[0, :].partition_broadcast(P))
+        age_rows = held.tile([BLOCKS, P], F32, name="age_rows")
+        nc.scalar.dma_start(age_rows[:], age.rearrange("(i p) one -> i (p one)", p=P))
+        female_rows = held.tile([BLOCKS, P], F32, name="female_rows")
+        nc.scalar.dma_start(female_rows[:], female.rearrange("(i p) one -> i (p one)", p=P))
+
+        identity = held.tile([P, P], F32, name="identity")
+        make_identity(nc, identity[:])
+
+        minus_center = held.tile([P, D_TILES], F32, name="minus_center")
+        nc.vector.tensor_scalar_mul(minus_center[:], center_cols[:], -1.0)
+
+        covariates = held.tile([BLOCKS, P], F32, name="covariates")
+        nc.vector.tensor_scalar(
+            covariates[:], age_rows[:], w2_rows[:BLOCKS, K : K + 1], b2_rows[:BLOCKS, :], op0=MULT, op1=ADD
+        )
+        female_term = held.tile([BLOCKS, P], F32, name="female_term")
+        nc.vector.tensor_scalar_mul(female_term[:], female_rows[:], w2_rows[:BLOCKS, K + 1 : K + 2])
+        nc.vector.tensor_tensor(covariates[:], covariates[:], female_term[:], ADD)
+
+        centred = [[None] * D_TILES for half in range(2)]
+
+        def load_and_centre_xt(half, group):
+            xt_raw = ring.tile([P, XT_TILES, XT_COLS], F32, tag="slot", name="xt_raw")
+            nc.sync.dma_start(
+                xt_raw[:],
+                xt_rows[:, group * XT_TILES : (group + 1) * XT_TILES, half * XT_COLS : (half + 1) * XT_COLS],
+            )
+            for j in range(XT_TILES):
+                t = group * XT_TILES + j
+                centred[half][t] = held.tile([P, XT_COLS], BF16, name=f"centred{half}_{t}")
+                nc.scalar.activation(centred[half][t][:], xt_raw[:, j, :], IDENTITY, bias=minus_center[:, t : t + 1])
+
+        def load_w1(pair):
+            w1_pair = ring.tile([P, W1_COLS], F32, tag="slot", name=f"w1_pair{pair}")
+            nc.sync.dma_start(w1_pair[:], w1[0, pair * W1_COLS : (pair + 1) * W1_COLS].partition_broadcast(P))
+            return w1_pair
+
+        rotation_bf = []
+        for t in range(D_TILES):
+            if t % XT_TILES == 0:
+                load_and_centre_xt(0, t // XT_TILES)
+            rotation_raw = ring.tile([P, S], F32, tag="slot", name="rotation_raw")
+            nc.sync.dma_start(rotation_raw[:], rotation_rows[:, t, :])
+            rotation_bf.append(held.tile([P, S], BF16, name=f"rotation_bf{t}"))
+            for c in range(BANKS):
+                cols = slice(c * BANK, (c + 1) * BANK)
+                if c % 2 == 0:
+                    nc.vector.tensor_copy(rotation_bf[t][:, cols], rotation_raw[:, cols])
+                else:
+                    nc.scalar.activation(rotation_bf[t][:, cols], rotation_raw[:, cols], COPY)
+
+        w1_rows = [load_w1(0), load_w1(1)]
+        for group in range(D_TILES // XT_TILES):
+            load_and_centre_xt(1, group)
+        w1_rows += [load_w1(2), load_w1(3)]
+
+        p_tiles = []
+        for i in range(BLOCKS):
+            p_tiles.append(held.tile([P, S], F32, name=f"p{i}"))
+            samples = slice((i % 2) * P, (i % 2 + 1) * P)
+            for c in range(BANKS):
+                cols = slice(c * BANK, (c + 1) * BANK)
+                bank = banks.tile([P, BANK], F32, tag="bank", name="bank")
+                for t in range(D_TILES):
+                    nc.tensor.matmul(
+                        bank[:],
+                        centred[i // 2][t][:, samples],
+                        rotation_bf[t][:, cols],
+                        start=(t == 0),
+                        stop=(t == D_TILES - 1),
+                    )
+                if i == 0 and c % 2 == 0:
+                    nc.vector.tensor_copy(p_tiles[i][:, cols], bank[:])
+                else:
+                    nc.scalar.activation(p_tiles[i][:, cols], bank[:], COPY)
+
+        sums = held.tile([P, BLOCKS, K], F32, name="sums")
+        for i in range(BLOCKS):
+            for k in range(K):
+                product = products.tile([P, H], F32, name="product")
+                nc.vector.tensor_tensor(
+                    product[:],
+                    p_tiles[i][:].indirect(offsets[:, k * (H // 16) : (k + 1) * (H // 16)]),
+                    w1_rows[k // 2][:, (k % 2) * H : (k % 2 + 1) * H],
+                    MULT,
+                )
+                nc.scalar.activation(product[:], product[:], COPY, accum_out=sums[:, i, k : k + 1])
+
+        u = held.tile([P, BLOCKS, K], F32, name="u")
+        nc.vector.tensor_tensor(u[:], sums[:], b1_rows[:].unsqueeze(1).to_broadcast([P, BLOCKS, K]), ADD)
+        nc.vector.tensor_tensor(u[:], u[:], w2_rows[:, 0:K].unsqueeze(1).to_broadcast([P, BLOCKS, K]), MULT)
+        score = held.tile([P, BLOCKS], F32, name="score")
+        nc.vector.reduce_sum(score[:], u[:], axis=mybir.AxisListType.X)
+
+        score_t = banks.tile([P, BANK], F32, tag="bank", name="score_t")
+        nc.tensor.transpose(score_t[:BLOCKS, :P], score[:], identity[:])
+        result = held.tile([BLOCKS, P], F32, name="result")
+        nc.vector.tensor_tensor(result[:], score_t[:BLOCKS, :P], covariates[:], ADD)
+        nc.sync.dma_start(out.rearrange("(i p) one -> i (p one)", p=P), result[:])

@@ -21,6 +21,7 @@ XT_COLS = 2 * P
 XT_TILES = S // XT_COLS
 W1_COLS = S
 RING_SLOTS = N // W1_COLS + D_TILES // XT_TILES
+PRODUCT_SLOTS = 6
 
 FLOPS = 2 * B * D * S + 2 * B * N
 
@@ -33,7 +34,7 @@ def tile_pcgrimage_b_kernel(tc, xt, center, rotation, w1, b1, w2, b2, female, ag
     with (
         tc.tile_pool(name="held", bufs=1) as held,
         tc.tile_pool(name="ring", bufs=RING_SLOTS) as ring,
-        tc.tile_pool(name="products", bufs=3) as products,
+        tc.tile_pool(name="products", bufs=PRODUCT_SLOTS) as products,
         tc.psum_pool(name="banks", bufs=8) as banks,
     ):
         offsets = held.tile([P, N // 16], U16, name="offsets")

@@ -21,7 +21,6 @@ XT_COLS = 2 * P
 XT_TILES = S // XT_COLS
 W1_COLS = S
 RING_SLOTS = N // W1_COLS + D_TILES // XT_TILES
-PRODUCT_SLOTS = 6
 
 FLOPS = 2 * B * D * S + 2 * B * N
 
@@ -34,7 +33,7 @@ def tile_pcgrimage_b_kernel(tc, xt, center, rotation, w1, b1, w2, b2, female, ag
     with (
         tc.tile_pool(name="held", bufs=1) as held,
         tc.tile_pool(name="ring", bufs=RING_SLOTS) as ring,
-        tc.tile_pool(name="products", bufs=PRODUCT_SLOTS) as products,
+        tc.tile_pool(name="products", bufs=3) as products,
         tc.psum_pool(name="banks", bufs=8) as banks,
     ):
         offsets = held.tile([P, N // 16], U16, name="offsets")
@@ -99,8 +98,9 @@ def tile_pcgrimage_b_kernel(tc, xt, center, rotation, w1, b1, w2, b2, female, ag
                 else:
                     nc.scalar.activation(rotation_bf[t][:, cols], rotation_raw[:, cols], COPY)
 
-        w1_rows = [load_w1(0), load_w1(1)]
+        w1_rows = []
         for group in range(D_TILES // XT_TILES):
+            w1_rows.append(load_w1(group))
             load_and_centre_xt(1, group)
         w1_rows += [load_w1(2), load_w1(3)]
 
@@ -119,7 +119,7 @@ def tile_pcgrimage_b_kernel(tc, xt, center, rotation, w1, b1, w2, b2, female, ag
                         start=(t == 0),
                         stop=(t == D_TILES - 1),
                     )
-                if i == 0 and c % 2 == 0:
+                if (i == 0 and c % 2 == 0) or (i == BLOCKS - 1 and c == BANKS - 1):
                     nc.vector.tensor_copy(p_tiles[i][:, cols], bank[:])
                 else:
                     nc.scalar.activation(p_tiles[i][:, cols], bank[:], COPY)

@@ -22,6 +22,9 @@ XT_TILES = S // XT_COLS
 W1_COLS = S
 RING_SLOTS = N // W1_COLS + D_TILES // XT_TILES
 
+PIECES = [(k * H, H) for k in range(K)]
+LAST_PIECES = PIECES[:-1] + [(N - H, H // 2), (N - H // 2, H // 4), (N - H // 4, H // 4)]
+
 FLOPS = 2 * B * D * S + 2 * B * N
 
 
@@ -58,9 +61,15 @@ def tile_pcgrimage_b_kernel(tc, xt, center, rotation, w1, b1, w2, b2, female, ag
         minus_center = held.tile([P, D_TILES], F32, name="minus_center")
         nc.vector.tensor_scalar_mul(minus_center[:], center_cols[:], -1.0)
 
+        b1_w2 = held.tile([BLOCKS, K], F32, name="b1_w2")
+        nc.vector.tensor_tensor(b1_w2[:], b1_rows[:BLOCKS, :], w2_rows[:BLOCKS, 0:K], MULT)
+        constant = held.tile([BLOCKS, 1], F32, name="constant")
+        nc.vector.reduce_sum(constant[:], b1_w2[:], axis=mybir.AxisListType.X)
+        nc.vector.tensor_tensor(constant[:], constant[:], b2_rows[:BLOCKS, :], ADD)
+
         covariates = held.tile([BLOCKS, P], F32, name="covariates")
         nc.vector.tensor_scalar(
-            covariates[:], age_rows[:], w2_rows[:BLOCKS, K : K + 1], b2_rows[:BLOCKS, :], op0=MULT, op1=ADD
+            covariates[:], age_rows[:], w2_rows[:BLOCKS, K : K + 1], constant[:], op0=MULT, op1=ADD
         )
         female_term = held.tile([BLOCKS, P], F32, name="female_term")
         nc.vector.tensor_scalar_mul(female_term[:], female_rows[:], w2_rows[:BLOCKS, K + 1 : K + 2])
@@ -124,23 +133,28 @@ def tile_pcgrimage_b_kernel(tc, xt, center, rotation, w1, b1, w2, b2, female, ag
                 else:
                     nc.scalar.activation(p_tiles[i][:, cols], bank[:], COPY)
 
-        sums = held.tile([P, BLOCKS, K], F32, name="sums")
+        sums = held.tile([P, BLOCKS, len(LAST_PIECES)], F32, name="sums")
+        nc.vector.memset(sums[:], 0.0)
         for i in range(BLOCKS):
-            for k in range(K):
+            for column, (first, entries) in enumerate(LAST_PIECES if i == BLOCKS - 1 else PIECES):
+                k = first // H
                 product = products.tile([P, H], F32, name="product")
                 nc.vector.tensor_tensor(
-                    product[:],
-                    p_tiles[i][:].indirect(offsets[:, k * (H // 16) : (k + 1) * (H // 16)]),
-                    w1_rows[k // 2][:, (k % 2) * H : (k % 2 + 1) * H],
+                    product[:, :entries],
+                    p_tiles[i][:].indirect(offsets[:, first // 16 : (first + entries) // 16]),
+                    w1_rows[first // W1_COLS][:, first % W1_COLS : first % W1_COLS + entries],
                     MULT,
                 )
-                nc.scalar.activation(product[:], product[:], COPY, accum_out=sums[:, i, k : k + 1])
+                nc.scalar.activation(
+                    product[:, :entries],
+                    product[:, :entries],
+                    COPY,
+                    scale=w2_rows[:, k : k + 1],
+                    accum_out=sums[:, i, column : column + 1],
+                )
 
-        u = held.tile([P, BLOCKS, K], F32, name="u")
-        nc.vector.tensor_tensor(u[:], sums[:], b1_rows[:].unsqueeze(1).to_broadcast([P, BLOCKS, K]), ADD)
-        nc.vector.tensor_tensor(u[:], u[:], w2_rows[:, 0:K].unsqueeze(1).to_broadcast([P, BLOCKS, K]), MULT)
         score = held.tile([P, BLOCKS], F32, name="score")
-        nc.vector.reduce_sum(score[:], u[:], axis=mybir.AxisListType.X)
+        nc.vector.reduce_sum(score[:], sums[:], axis=mybir.AxisListType.X)
 
         score_t = banks.tile([P, BANK], F32, tag="bank", name="score_t")
         nc.tensor.transpose(score_t[:BLOCKS, :P], score[:], identity[:])

@@ -97,12 +97,16 @@ def tile_pcgrimage_b_kernel(tc, xt, center, rotation, w1, b1, w2, b2, female, ag
         for t in range(D_TILES):
             if t % XT_TILES == 0:
                 load_and_centre_xt(0, t // XT_TILES)
+            last = t == D_TILES - 1
             rotation_raw = ring.tile([P, S], F32, tag="slot", name="rotation_raw")
-            nc.sync.dma_start(rotation_raw[:], rotation_rows[:, t, :])
+            if not last:
+                nc.sync.dma_start(rotation_raw[:], rotation_rows[:, t, :])
             rotation_bf.append(held.tile([P, S], BF16, name=f"rotation_bf{t}"))
             for c in range(BANKS):
                 cols = slice(c * BANK, (c + 1) * BANK)
-                if c % 2 == 0:
+                if last:
+                    nc.sync.dma_start(rotation_raw[:, cols], rotation_rows[:, t, cols])
+                if c % 2 == 0 or last:
                     nc.vector.tensor_copy(rotation_bf[t][:, cols], rotation_raw[:, cols])
                 else:
                     nc.scalar.activation(rotation_bf[t][:, cols], rotation_raw[:, cols], COPY)
@@ -128,7 +132,7 @@ def tile_pcgrimage_b_kernel(tc, xt, center, rotation, w1, b1, w2, b2, female, ag
                         start=(t == 0),
                         stop=(t == D_TILES - 1),
                     )
-                if (i == 0 and c % 2 == 0) or (i == BLOCKS - 1 and c == BANKS - 1):
+                if (i == 0 or i == BLOCKS - 1) and c == BANKS - 1:
                     nc.vector.tensor_copy(p_tiles[i][:, cols], bank[:])
                 else:
                     nc.scalar.activation(p_tiles[i][:, cols], bank[:], COPY)

@@ -17,10 +17,8 @@ D_TILES = D // P
 BLOCKS = B // P
 BANK = 512
 BANKS = S // BANK
-XT_COLS = 2 * P
-XT_TILES = S // XT_COLS
-W1_COLS = S
-RING_SLOTS = N // W1_COLS + D_TILES // XT_TILES
+QUARTER_TILES = D_TILES // 4
+RING_SLOTS = 6
 
 PIECES = [(k * H, H) for k in range(K)]
 LAST_PIECES = PIECES[:-1] + [(N - H, H // 2), (N - H // 2, H // 4), (N - H // 4, H // 4)]
@@ -39,27 +37,24 @@ def tile_pcgrimage_b_kernel(tc, xt, center, rotation, w1, b1, w2, b2, female, ag
         tc.tile_pool(name="products", bufs=3) as products,
         tc.psum_pool(name="banks", bufs=8) as banks,
     ):
-        offsets = held.tile([P, N // 16], U16, name="offsets")
-        nc.sync.dma_start(offsets[:], offs)
-
         center_cols = held.tile([P, D_TILES], F32, name="center_cols")
-        nc.scalar.dma_start(center_cols[:], center.rearrange("(p t) one -> p (t one)", t=D_TILES))
+        nc.sync.dma_start(center_cols[:], center.rearrange("(p t) one -> p (t one)", t=D_TILES))
         b1_rows = held.tile([P, K], F32, name="b1_rows")
-        nc.scalar.dma_start(b1_rows[:], b1[0, :].partition_broadcast(P))
+        nc.sync.dma_start(b1_rows[:], b1[0, :].partition_broadcast(P))
         w2_rows = held.tile([P, K + 2], F32, name="w2_rows")
-        nc.scalar.dma_start(w2_rows[:], w2[0, :].partition_broadcast(P))
+        nc.sync.dma_start(w2_rows[:], w2[0, :].partition_broadcast(P))
         b2_rows = held.tile([P, 1], F32, name="b2_rows")
-        nc.scalar.dma_start(b2_rows[:], b2[0, :].partition_broadcast(P))
+        nc.sync.dma_start(b2_rows[:], b2[0, :].partition_broadcast(P))
         age_rows = held.tile([BLOCKS, P], F32, name="age_rows")
-        nc.scalar.dma_start(age_rows[:], age.rearrange("(i p) one -> i (p one)", p=P))
+        nc.sync.dma_start(age_rows[:], age.rearrange("(i p) one -> i (p one)", p=P))
         female_rows = held.tile([BLOCKS, P], F32, name="female_rows")
-        nc.scalar.dma_start(female_rows[:], female.rearrange("(i p) one -> i (p one)", p=P))
+        nc.sync.dma_start(female_rows[:], female.rearrange("(i p) one -> i (p one)", p=P))
 
         identity = held.tile([P, P], F32, name="identity")
         make_identity(nc, identity[:])
 
         minus_center = held.tile([P, D_TILES], F32, name="minus_center")
-        nc.vector.tensor_scalar_mul(minus_center[:], center_cols[:], -1.0)
+        nc.scalar.mul(minus_center[:], center_cols[:], -1.0)
 
         b1_w2 = held.tile([BLOCKS, K], F32, name="b1_w2")
         nc.vector.tensor_tensor(b1_w2[:], b1_rows[:BLOCKS, :], w2_rows[:BLOCKS, 0:K], MULT)
@@ -75,28 +70,33 @@ def tile_pcgrimage_b_kernel(tc, xt, center, rotation, w1, b1, w2, b2, female, ag
         nc.vector.tensor_scalar_mul(female_term[:], female_rows[:], w2_rows[:BLOCKS, K + 1 : K + 2])
         nc.vector.tensor_tensor(covariates[:], covariates[:], female_term[:], ADD)
 
-        centred = [[None] * D_TILES for half in range(2)]
+        centred = [[None] * D_TILES for i in range(BLOCKS)]
 
-        def load_and_centre_xt(half, group):
-            xt_raw = ring.tile([P, XT_TILES, XT_COLS], F32, tag="slot", name="xt_raw")
+        def load_and_centre_xt(first_block, blocks, first_tile, tiles):
+            columns = blocks * P
+            xt_raw = ring.tile([P, tiles, columns], F32, tag="slot", name="xt_raw")
             nc.sync.dma_start(
                 xt_raw[:],
-                xt_rows[:, group * XT_TILES : (group + 1) * XT_TILES, half * XT_COLS : (half + 1) * XT_COLS],
+                xt_rows[:, first_tile : first_tile + tiles, first_block * P : first_block * P + columns],
             )
-            for j in range(XT_TILES):
-                t = group * XT_TILES + j
-                centred[half][t] = held.tile([P, XT_COLS], BF16, name=f"centred{half}_{t}")
-                nc.scalar.activation(centred[half][t][:], xt_raw[:, j, :], IDENTITY, bias=minus_center[:, t : t + 1])
+            for t in range(first_tile, first_tile + tiles):
+                centred_t = held.tile([P, columns], BF16, name=f"centred{first_block}_{t}")
+                nc.scalar.activation(
+                    centred_t[:], xt_raw[:, t - first_tile, :], IDENTITY, bias=minus_center[:, t : t + 1]
+                )
+                for i in range(blocks):
+                    centred[first_block + i][t] = centred_t[:, i * P : (i + 1) * P]
 
-        def load_w1(pair):
-            w1_pair = ring.tile([P, W1_COLS], F32, tag="slot", name=f"w1_pair{pair}")
-            nc.sync.dma_start(w1_pair[:], w1[0, pair * W1_COLS : (pair + 1) * W1_COLS].partition_broadcast(P))
-            return w1_pair
+        w1_rows = held.tile([P, N], F32, name="w1_rows")
+
+        def load_w1(k):
+            entries = slice(k * H, (k + 1) * H)
+            nc.sync.dma_start(w1_rows[:, entries], w1[0, entries].partition_broadcast(P))
 
         rotation_bf = []
         for t in range(D_TILES):
-            if t % XT_TILES == 0:
-                load_and_centre_xt(0, t // XT_TILES)
+            if t % QUARTER_TILES == 0:
+                load_and_centre_xt(0, 2, t, QUARTER_TILES)
             last = t == D_TILES - 1
             rotation_raw = ring.tile([P, S], F32, tag="slot", name="rotation_raw")
             if not last:
@@ -111,23 +111,24 @@ def tile_pcgrimage_b_kernel(tc, xt, center, rotation, w1, b1, w2, b2, female, ag
                 else:
                     nc.scalar.activation(rotation_bf[t][:, cols], rotation_raw[:, cols], COPY)
 
-        w1_rows = []
-        for group in range(D_TILES // XT_TILES):
-            w1_rows.append(load_w1(group))
-            load_and_centre_xt(1, group)
-        w1_rows += [load_w1(2), load_w1(3)]
+        offsets = held.tile([P, N // 16], U16, name="offsets")
+        nc.sync.dma_start(offsets[:], offs)
+        for k in range(K):
+            load_w1(k)
+            if k * QUARTER_TILES < D_TILES:
+                load_and_centre_xt(2, 1, k * QUARTER_TILES, QUARTER_TILES)
+        load_and_centre_xt(3, 1, 0, D_TILES)
 
         p_tiles = []
         for i in range(BLOCKS):
             p_tiles.append(held.tile([P, S], F32, name=f"p{i}"))
-            samples = slice((i % 2) * P, (i % 2 + 1) * P)
             for c in range(BANKS):
                 cols = slice(c * BANK, (c + 1) * BANK)
                 bank = banks.tile([P, BANK], F32, tag="bank", name="bank")
                 for t in range(D_TILES):
                     nc.tensor.matmul(
                         bank[:],
-                        centred[i // 2][t][:, samples],
+                        centred[i][t],
                         rotation_bf[t][:, cols],
                         start=(t == 0),
                         stop=(t == D_TILES - 1),
@@ -146,7 +147,7 @@ def tile_pcgrimage_b_kernel(tc, xt, center, rotation, w1, b1, w2, b2, female, ag
                 nc.vector.tensor_tensor(
                     product[:, :entries],
                     p_tiles[i][:].indirect(offsets[:, first // 16 : (first + entries) // 16]),
-                    w1_rows[first // W1_COLS][:, first % W1_COLS : first % W1_COLS + entries],
+                    w1_rows[:, first : first + entries],
                     MULT,
                 )
                 nc.scalar.activation(

@@ -18,6 +18,7 @@ BLOCKS = B // P
 BANK = 512
 BANKS = S // BANK
 QUARTER_TILES = D_TILES // 4
+HELD_BACK = 2
 RING_SLOTS = 6
 
 PIECES = [(k * H, H) for k in range(K)]
@@ -95,8 +96,11 @@ def tile_pcgrimage_b_kernel(tc, xt, center, rotation, w1, b1, w2, b2, female, ag
 
         rotation_bf = []
         for t in range(D_TILES):
-            if t % QUARTER_TILES == 0:
+            if t % QUARTER_TILES == 0 and t < D_TILES - QUARTER_TILES:
                 load_and_centre_xt(0, 2, t, QUARTER_TILES)
+            if t == D_TILES - QUARTER_TILES:
+                load_and_centre_xt(0, 2, t, QUARTER_TILES - HELD_BACK)
+                load_and_centre_xt(0, 1, D_TILES - HELD_BACK, HELD_BACK)
             last = t == D_TILES - 1
             rotation_raw = ring.tile([P, S], F32, tag="slot", name="rotation_raw")
             if not last:
@@ -113,10 +117,13 @@ def tile_pcgrimage_b_kernel(tc, xt, center, rotation, w1, b1, w2, b2, female, ag
 
         offsets = held.tile([P, N // 16], U16, name="offsets")
         nc.sync.dma_start(offsets[:], offs)
+        late_xt = [(1, D_TILES - HELD_BACK, HELD_BACK)]
+        late_xt += [(2, first_tile, QUARTER_TILES) for first_tile in range(0, D_TILES, QUARTER_TILES)]
         for k in range(K):
             load_w1(k)
-            if k * QUARTER_TILES < D_TILES:
-                load_and_centre_xt(2, 1, k * QUARTER_TILES, QUARTER_TILES)
+            if k < len(late_xt):
+                i, first_tile, tiles = late_xt[k]
+                load_and_centre_xt(i, 1, first_tile, tiles)
         load_and_centre_xt(3, 1, 0, D_TILES)
 
         p_tiles = []

@@ -39,17 +39,17 @@ def tile_pcgrimage_b_kernel(tc, xt, center, rotation, w1, b1, w2, b2, female, ag
         tc.psum_pool(name="banks", bufs=8) as banks,
     ):
         center_cols = held.tile([P, D_TILES], F32, name="center_cols")
-        nc.sync.dma_start(center_cols[:], center.rearrange("(p t) one -> p (t one)", t=D_TILES))
+        nc.scalar.dma_start(center_cols[:], center.rearrange("(p t) one -> p (t one)", t=D_TILES))
         b1_rows = held.tile([P, K], F32, name="b1_rows")
-        nc.sync.dma_start(b1_rows[:], b1[0, :].partition_broadcast(P))
+        nc.scalar.dma_start(b1_rows[:], b1[0, :].partition_broadcast(P))
         w2_rows = held.tile([P, K + 2], F32, name="w2_rows")
-        nc.sync.dma_start(w2_rows[:], w2[0, :].partition_broadcast(P))
+        nc.scalar.dma_start(w2_rows[:], w2[0, :].partition_broadcast(P))
         b2_rows = held.tile([P, 1], F32, name="b2_rows")
-        nc.sync.dma_start(b2_rows[:], b2[0, :].partition_broadcast(P))
+        nc.scalar.dma_start(b2_rows[:], b2[0, :].partition_broadcast(P))
         age_rows = held.tile([BLOCKS, P], F32, name="age_rows")
-        nc.sync.dma_start(age_rows[:], age.rearrange("(i p) one -> i (p one)", p=P))
+        nc.scalar.dma_start(age_rows[:], age.rearrange("(i p) one -> i (p one)", p=P))
         female_rows = held.tile([BLOCKS, P], F32, name="female_rows")
-        nc.sync.dma_start(female_rows[:], female.rearrange("(i p) one -> i (p one)", p=P))
+        nc.scalar.dma_start(female_rows[:], female.rearrange("(i p) one -> i (p one)", p=P))
 
         identity = held.tile([P, P], F32, name="identity")
         make_identity(nc, identity[:])

@@ -18,7 +18,7 @@ BLOCKS = B // P
 BANK = 512
 BANKS = S // BANK
 QUARTER_TILES = D_TILES // 4
-HELD_BACK = 2
+EARLY_TILES = QUARTER_TILES
 RING_SLOTS = 6
 
 PIECES = [(k * H, H) for k in range(K)]
@@ -40,36 +40,24 @@ def tile_pcgrimage_b_kernel(tc, xt, center, rotation, w1, b1, w2, b2, female, ag
     ):
         center_cols = held.tile([P, D_TILES], F32, name="center_cols")
         nc.scalar.dma_start(center_cols[:], center.rearrange("(p t) one -> p (t one)", t=D_TILES))
-        b1_rows = held.tile([P, K], F32, name="b1_rows")
-        nc.scalar.dma_start(b1_rows[:], b1[0, :].partition_broadcast(P))
-        w2_rows = held.tile([P, K + 2], F32, name="w2_rows")
-        nc.scalar.dma_start(w2_rows[:], w2[0, :].partition_broadcast(P))
-        b2_rows = held.tile([P, 1], F32, name="b2_rows")
-        nc.scalar.dma_start(b2_rows[:], b2[0, :].partition_broadcast(P))
-        age_rows = held.tile([BLOCKS, P], F32, name="age_rows")
-        nc.scalar.dma_start(age_rows[:], age.rearrange("(i p) one -> i (p one)", p=P))
-        female_rows = held.tile([BLOCKS, P], F32, name="female_rows")
-        nc.scalar.dma_start(female_rows[:], female.rearrange("(i p) one -> i (p one)", p=P))
+        minus_center = held.tile([P, D_TILES], F32, name="minus_center")
+        nc.scalar.mul(minus_center[:], center_cols[:], -1.0)
 
         identity = held.tile([P, P], F32, name="identity")
         make_identity(nc, identity[:])
 
-        minus_center = held.tile([P, D_TILES], F32, name="minus_center")
-        nc.scalar.mul(minus_center[:], center_cols[:], -1.0)
+        b1_rows = held.tile([P, K], F32, name="b1_rows")
+        w2_rows = held.tile([P, K + 2], F32, name="w2_rows")
+        b2_rows = held.tile([P, 1], F32, name="b2_rows")
+        age_rows = held.tile([BLOCKS, P], F32, name="age_rows")
+        female_rows = held.tile([BLOCKS, P], F32, name="female_rows")
 
-        b1_w2 = held.tile([BLOCKS, K], F32, name="b1_w2")
-        nc.vector.tensor_tensor(b1_w2[:], b1_rows[:BLOCKS, :], w2_rows[:BLOCKS, 0:K], MULT)
-        constant = held.tile([BLOCKS, 1], F32, name="constant")
-        nc.vector.reduce_sum(constant[:], b1_w2[:], axis=mybir.AxisListType.X)
-        nc.vector.tensor_tensor(constant[:], constant[:], b2_rows[:BLOCKS, :], ADD)
-
-        covariates = held.tile([BLOCKS, P], F32, name="covariates")
-        nc.vector.tensor_scalar(
-            covariates[:], age_rows[:], w2_rows[:BLOCKS, K : K + 1], constant[:], op0=MULT, op1=ADD
-        )
-        female_term = held.tile([BLOCKS, P], F32, name="female_term")
-        nc.vector.tensor_scalar_mul(female_term[:], female_rows[:], w2_rows[:BLOCKS, K + 1 : K + 2])
-        nc.vector.tensor_tensor(covariates[:], covariates[:], female_term[:], ADD)
+        def load_small_inputs():
+            nc.sync.dma_start(b1_rows[:], b1[0, :].partition_broadcast(P))
+            nc.sync.dma_start(w2_rows[:], w2[0, :].partition_broadcast(P))
+            nc.sync.dma_start(b2_rows[:], b2[0, :].partition_broadcast(P))
+            nc.sync.dma_start(age_rows[:], age.rearrange("(i p) one -> i (p one)", p=P))
+            nc.sync.dma_start(female_rows[:], female.rearrange("(i p) one -> i (p one)", p=P))
 
         centred = [[None] * D_TILES for i in range(BLOCKS)]
 
@@ -96,11 +84,10 @@ def tile_pcgrimage_b_kernel(tc, xt, center, rotation, w1, b1, w2, b2, female, ag
 
         rotation_bf = []
         for t in range(D_TILES):
-            if t % QUARTER_TILES == 0 and t < D_TILES - QUARTER_TILES:
-                load_and_centre_xt(0, 2, t, QUARTER_TILES)
-            if t == D_TILES - QUARTER_TILES:
-                load_and_centre_xt(0, 2, t, QUARTER_TILES - HELD_BACK)
-                load_and_centre_xt(0, 1, D_TILES - HELD_BACK, HELD_BACK)
+            if t % QUARTER_TILES == 0:
+                load_and_centre_xt(0, 2 if t < EARLY_TILES else 1, t, QUARTER_TILES)
+            if t == QUARTER_TILES:
+                load_small_inputs()
             last = t == D_TILES - 1
             rotation_raw = ring.tile([P, S], F32, tag="slot", name="rotation_raw")
             if not last:
@@ -117,14 +104,31 @@ def tile_pcgrimage_b_kernel(tc, xt, center, rotation, w1, b1, w2, b2, female, ag
 
         offsets = held.tile([P, N // 16], U16, name="offsets")
         nc.sync.dma_start(offsets[:], offs)
-        late_xt = [(1, D_TILES - HELD_BACK, HELD_BACK)]
-        late_xt += [(2, first_tile, QUARTER_TILES) for first_tile in range(0, D_TILES, QUARTER_TILES)]
-        for k in range(K):
+        for k in range(K - 1):
             load_w1(k)
-            if k < len(late_xt):
-                i, first_tile, tiles = late_xt[k]
-                load_and_centre_xt(i, 1, first_tile, tiles)
+            first_tile = EARLY_TILES + k * QUARTER_TILES
+            if first_tile < D_TILES:
+                load_and_centre_xt(1, 1, first_tile, QUARTER_TILES)
+        load_and_centre_xt(2, 1, 0, D_TILES)
+        load_w1(K - 1)
         load_and_centre_xt(3, 1, 0, D_TILES)
+
+        b1_w2 = held.tile([BLOCKS, K], F32, name="b1_w2")
+        nc.gpsimd.tensor_tensor(b1_w2[:], b1_rows[:BLOCKS, :], w2_rows[:BLOCKS, 0:K], MULT)
+        b1_share = held.tile([BLOCKS, 1], F32, name="b1_share")
+        nc.scalar.activation(b1_w2[:], b1_w2[:], COPY, accum_out=b1_share[:])
+        constant = held.tile([BLOCKS, 1], F32, name="constant")
+        nc.gpsimd.tensor_tensor(constant[:], b1_share[:], b2_rows[:BLOCKS, :], ADD)
+
+        age_term = held.tile([BLOCKS, P], F32, name="age_term")
+        nc.gpsimd.tensor_scalar(age_term[:], age_rows[:], w2_rows[:BLOCKS, K : K + 1], constant[:], op0=MULT, op1=ADD)
+        female_term = held.tile([BLOCKS, P], F32, name="female_term")
+        nc.gpsimd.tensor_scalar(female_term[:], female_rows[:], w2_rows[:BLOCKS, K + 1 : K + 2], None, op0=MULT)
+        covariates = held.tile([BLOCKS, P], F32, name="covariates")
+        nc.gpsimd.tensor_tensor(covariates[:], age_term[:], female_term[:], ADD)
+
+        sums = held.tile([P, BLOCKS, len(LAST_PIECES)], F32, name="sums")
+        nc.vector.memset(sums[:], 0.0)
 
         p_tiles = []
         for i in range(BLOCKS):
@@ -140,13 +144,14 @@ def tile_pcgrimage_b_kernel(tc, xt, center, rotation, w1, b1, w2, b2, female, ag
                         start=(t == 0),
                         stop=(t == D_TILES - 1),
                     )
-                if (i == 0 or i == BLOCKS - 1) and c == BANKS - 1:
+                if i == 0 and c == BANKS - 1:
                     nc.vector.tensor_copy(p_tiles[i][:, cols], bank[:])
-                else:
+                elif i == 0:
                     nc.scalar.activation(p_tiles[i][:, cols], bank[:], COPY)
+                else:
+                    placeholder = sums[:, i - 1, K - BANKS + c : K - BANKS + c + 1]
+                    nc.scalar.activation(p_tiles[i][:, cols], bank[:], COPY, accum_out=placeholder)
 
-        sums = held.tile([P, BLOCKS, len(LAST_PIECES)], F32, name="sums")
-        nc.vector.memset(sums[:], 0.0)
         for i in range(BLOCKS):
             for column, (first, entries) in enumerate(LAST_PIECES if i == BLOCKS - 1 else PIECES):
                 k = first // H

@@ -6,6 +6,7 @@ BF16 = mybir.dt.bfloat16
 U16 = mybir.dt.uint16
 ADD = mybir.AluOpType.add
 MULT = mybir.AluOpType.mult
+SUBTRACT = mybir.AluOpType.subtract
 COPY = mybir.ActivationFunctionType.Copy
 IDENTITY = mybir.ActivationFunctionType.Identity
 
@@ -17,6 +18,8 @@ D_TILES = D // P
 BLOCKS = B // P
 BANK = 512
 BANKS = S // BANK
+W1_ROWS = N // BANK
+QUADRANT = 32
 QUARTER_TILES = D_TILES // 4
 EARLY_TILES = QUARTER_TILES
 RING_SLOTS = 6
@@ -45,6 +48,42 @@ def tile_pcgrimage_b_kernel(tc, xt, center, rotation, w1, b1, w2, b2, female, ag
 
         identity = held.tile([P, P], F32, name="identity")
         make_identity(nc, identity[:])
+
+        w1_stack = held.tile([P, BANK], F32, name="w1_stack")
+        nc.vector.memset(w1_stack[:], 0.0)
+        for first in (0, QUADRANT, 2 * QUADRANT):
+            nc.sync.dma_start(w1_stack[first : first + W1_ROWS, :], w1.rearrange("one (c n) -> (one c) n", n=BANK))
+        w1_parts = held.tile([P, BANK], BF16, name="w1_parts")
+        nc.vector.tensor_copy(w1_parts[:], w1_stack[:])
+        below_upper = held.tile([P, BANK], F32, name="below_upper")
+        nc.vector.tensor_tensor(below_upper[:], w1_stack[:], w1_parts[:], SUBTRACT)
+        middle = held.tile([P, BANK], BF16, name="middle")
+        nc.vector.tensor_copy(middle[:], below_upper[:])
+        below_middle = held.tile([P, BANK], F32, name="below_middle")
+        nc.vector.tensor_tensor(below_middle[:], below_upper[:], middle[:], SUBTRACT)
+        second, third = slice(QUADRANT, 2 * QUADRANT), slice(2 * QUADRANT, 3 * QUADRANT)
+        nc.vector.tensor_copy(w1_parts[second, :], middle[second, :])
+        nc.vector.tensor_copy(w1_parts[third, :], below_middle[third, :])
+
+        pick_two = held.tile([P, W1_ROWS], F32, name="pick_two")
+        nc.vector.tensor_tensor(
+            pick_two[:], identity[:, 0:W1_ROWS], identity[:, QUADRANT : QUADRANT + W1_ROWS], ADD
+        )
+        pick_three = held.tile([P, W1_ROWS], F32, name="pick_three")
+        nc.vector.tensor_tensor(
+            pick_three[:], pick_two[:], identity[:, 2 * QUADRANT : 2 * QUADRANT + W1_ROWS], ADD
+        )
+        pick = held.tile([P, W1_ROWS, P], BF16, name="pick")
+        nc.vector.tensor_copy(pick[:], pick_three[:].unsqueeze(2).to_broadcast([P, W1_ROWS, P]))
+
+        w1_rows = held.tile([P, N], F32, name="w1_rows")
+        for c in range(W1_ROWS):
+            spread = banks.tile([P, BANK], F32, tag="bank", name="spread")
+            nc.tensor.matmul(spread[:], pick[:, c, :], w1_parts[:], start=True, stop=True)
+            if c % 2 == 0:
+                nc.vector.tensor_copy(w1_rows[:, c * BANK : (c + 1) * BANK], spread[:])
+            else:
+                nc.scalar.activation(w1_rows[:, c * BANK : (c + 1) * BANK], spread[:], COPY)
 
         b1_rows = held.tile([P, K], F32, name="b1_rows")
         w2_rows = held.tile([P, K + 2], F32, name="w2_rows")
@@ -76,12 +115,6 @@ def tile_pcgrimage_b_kernel(tc, xt, center, rotation, w1, b1, w2, b2, female, ag
                 for i in range(blocks):
                     centred[first_block + i][t] = centred_t[:, i * P : (i + 1) * P]
 
-        w1_rows = held.tile([P, N], F32, name="w1_rows")
-
-        def load_w1(k):
-            entries = slice(k * H, (k + 1) * H)
-            nc.sync.dma_start(w1_rows[:, entries], w1[0, entries].partition_broadcast(P))
-
         rotation_bf = []
         for t in range(D_TILES):
             if t % QUARTER_TILES == 0:
@@ -104,13 +137,9 @@ def tile_pcgrimage_b_kernel(tc, xt, center, rotation, w1, b1, w2, b2, female, ag
 
         offsets = held.tile([P, N // 16], U16, name="offsets")
         nc.sync.dma_start(offsets[:], offs)
-        for k in range(K - 1):
-            load_w1(k)
-            first_tile = EARLY_TILES + k * QUARTER_TILES
-            if first_tile < D_TILES:
-                load_and_centre_xt(1, 1, first_tile, QUARTER_TILES)
+        for first_tile in range(EARLY_TILES, D_TILES, QUARTER_TILES):
+            load_and_centre_xt(1, 1, first_tile, QUARTER_TILES)
         load_and_centre_xt(2, 1, 0, D_TILES)
-        load_w1(K - 1)
         load_and_centre_xt(3, 1, 0, D_TILES)
 
         b1_w2 = held.tile([BLOCKS, K], F32, name="b1_w2")

@@ -22,6 +22,7 @@ W1_ROWS = N // BANK
 QUADRANT = 32
 QUARTER_TILES = D_TILES // 4
 EARLY_TILES = QUARTER_TILES
+LATE_TILES = 2
 RING_SLOTS = 6
 
 PIECES = [(k * H, H) for k in range(K)]
@@ -137,10 +138,11 @@ def tile_pcgrimage_b_kernel(tc, xt, center, rotation, w1, b1, w2, b2, female, ag
 
         offsets = held.tile([P, N // 16], U16, name="offsets")
         nc.sync.dma_start(offsets[:], offs)
-        for first_tile in range(EARLY_TILES, D_TILES, QUARTER_TILES):
-            load_and_centre_xt(1, 1, first_tile, QUARTER_TILES)
-        load_and_centre_xt(2, 1, 0, D_TILES)
-        load_and_centre_xt(3, 1, 0, D_TILES)
+        for first_tile in range(EARLY_TILES, D_TILES, LATE_TILES):
+            load_and_centre_xt(1, 1, first_tile, LATE_TILES)
+        for i in (2, 3):
+            for first_tile in range(0, D_TILES, LATE_TILES):
+                load_and_centre_xt(i, 1, first_tile, LATE_TILES)
 
         b1_w2 = held.tile([BLOCKS, K], F32, name="b1_w2")
         nc.gpsimd.tensor_tensor(b1_w2[:], b1_rows[:BLOCKS, :], w2_rows[:BLOCKS, 0:K], MULT)

import concourse.mybir as mybir
from concourse.masks import make_identity

F32 = mybir.dt.float32
BF16 = mybir.dt.bfloat16
U16 = mybir.dt.uint16
ADD = mybir.AluOpType.add
MULT = mybir.AluOpType.mult
SUBTRACT = mybir.AluOpType.subtract
COPY = mybir.ActivationFunctionType.Copy
IDENTITY = mybir.ActivationFunctionType.Identity

P = 128
B, D, S = 512, 2048, 2048
K, H = 8, 1024
N = K * H
D_TILES = D // P
BLOCKS = B // P
BANK = 512
BANKS = S // BANK
W1_ROWS = N // BANK
QUADRANT = 32
QUARTER_TILES = D_TILES // 4
EARLY_TILES = QUARTER_TILES
LATE_TILES = 2
RING_SLOTS = 6

PIECES = [(k * H, H) for k in range(K)]
LAST_PIECES = PIECES[:-1] + [(N - H, H // 2), (N - H // 2, H // 4), (N - H // 4, H // 4)]

FLOPS = 2 * B * D * S + 2 * B * N


def tile_pcgrimage_b_kernel(tc, xt, center, rotation, w1, b1, w2, b2, female, age, offs, out):
    nc = tc.nc
    xt_rows = xt.rearrange("(p t) b -> p t b", t=D_TILES)
    rotation_rows = rotation.rearrange("(p t) s -> p t s", t=D_TILES)

    with (
        tc.tile_pool(name="held", bufs=1) as held,
        tc.tile_pool(name="ring", bufs=RING_SLOTS) as ring,
        tc.tile_pool(name="products", bufs=3) as products,
        tc.psum_pool(name="banks", bufs=8) as banks,
    ):
        center_cols = held.tile([P, D_TILES], F32, name="center_cols")
        nc.scalar.dma_start(center_cols[:], center.rearrange("(p t) one -> p (t one)", t=D_TILES))
        minus_center = held.tile([P, D_TILES], F32, name="minus_center")
        nc.scalar.mul(minus_center[:], center_cols[:], -1.0)

        identity = held.tile([P, P], F32, name="identity")
        make_identity(nc, identity[:])

        w1_stack = held.tile([P, BANK], F32, name="w1_stack")
        nc.vector.memset(w1_stack[:], 0.0)
        for first in (0, QUADRANT, 2 * QUADRANT):
            nc.sync.dma_start(w1_stack[first : first + W1_ROWS, :], w1.rearrange("one (c n) -> (one c) n", n=BANK))
        w1_parts = held.tile([P, BANK], BF16, name="w1_parts")
        nc.vector.tensor_copy(w1_parts[:], w1_stack[:])
        below_upper = held.tile([P, BANK], F32, name="below_upper")
        nc.vector.tensor_tensor(below_upper[:], w1_stack[:], w1_parts[:], SUBTRACT)
        middle = held.tile([P, BANK], BF16, name="middle")
        nc.vector.tensor_copy(middle[:], below_upper[:])
        below_middle = held.tile([P, BANK], F32, name="below_middle")
        nc.vector.tensor_tensor(below_middle[:], below_upper[:], middle[:], SUBTRACT)
        second, third = slice(QUADRANT, 2 * QUADRANT), slice(2 * QUADRANT, 3 * QUADRANT)
        nc.vector.tensor_copy(w1_parts[second, :], middle[second, :])
        nc.vector.tensor_copy(w1_parts[third, :], below_middle[third, :])

        pick_two = held.tile([P, W1_ROWS], F32, name="pick_two")
        nc.vector.tensor_tensor(
            pick_two[:], identity[:, 0:W1_ROWS], identity[:, QUADRANT : QUADRANT + W1_ROWS], ADD
        )
        pick_three = held.tile([P, W1_ROWS], F32, name="pick_three")
        nc.vector.tensor_tensor(
            pick_three[:], pick_two[:], identity[:, 2 * QUADRANT : 2 * QUADRANT + W1_ROWS], ADD
        )
        pick = held.tile([P, W1_ROWS, P], BF16, name="pick")
        nc.vector.tensor_copy(pick[:], pick_three[:].unsqueeze(2).to_broadcast([P, W1_ROWS, P]))

        w1_rows = held.tile([P, N], F32, name="w1_rows")
        for c in range(W1_ROWS):
            spread = banks.tile([P, BANK], F32, tag="bank", name="spread")
            nc.tensor.matmul(spread[:], pick[:, c, :], w1_parts[:], start=True, stop=True)
            if c % 2 == 0:
                nc.vector.tensor_copy(w1_rows[:, c * BANK : (c + 1) * BANK], spread[:])
            else:
                nc.scalar.activation(w1_rows[:, c * BANK : (c + 1) * BANK], spread[:], COPY)

        b1_rows = held.tile([P, K], F32, name="b1_rows")
        w2_rows = held.tile([P, K + 2], F32, name="w2_rows")
        b2_rows = held.tile([P, 1], F32, name="b2_rows")
        age_rows = held.tile([BLOCKS, P], F32, name="age_rows")
        female_rows = held.tile([BLOCKS, P], F32, name="female_rows")

        def load_small_inputs():
            nc.sync.dma_start(b1_rows[:], b1[0, :].partition_broadcast(P))
            nc.sync.dma_start(w2_rows[:], w2[0, :].partition_broadcast(P))
            nc.sync.dma_start(b2_rows[:], b2[0, :].partition_broadcast(P))
            nc.sync.dma_start(age_rows[:], age.rearrange("(i p) one -> i (p one)", p=P))
            nc.sync.dma_start(female_rows[:], female.rearrange("(i p) one -> i (p one)", p=P))

        centred = [[None] * D_TILES for i in range(BLOCKS)]

        def load_and_centre_xt(first_block, blocks, first_tile, tiles):
            columns = blocks * P
            xt_raw = ring.tile([P, tiles, columns], F32, tag="slot", name="xt_raw")
            nc.sync.dma_start(
                xt_raw[:],
                xt_rows[:, first_tile : first_tile + tiles, first_block * P : first_block * P + columns],
            )
            for t in range(first_tile, first_tile + tiles):
                centred_t = held.tile([P, columns], BF16, name=f"centred{first_block}_{t}")
                nc.scalar.activation(
                    centred_t[:], xt_raw[:, t - first_tile, :], IDENTITY, bias=minus_center[:, t : t + 1]
                )
                for i in range(blocks):
                    centred[first_block + i][t] = centred_t[:, i * P : (i + 1) * P]

        rotation_bf = []
        for t in range(D_TILES):
            if t % QUARTER_TILES == 0:
                load_and_centre_xt(0, 2 if t < EARLY_TILES else 1, t, QUARTER_TILES)
            if t == QUARTER_TILES:
                load_small_inputs()
            last = t == D_TILES - 1
            rotation_raw = ring.tile([P, S], F32, tag="slot", name="rotation_raw")
            if not last:
                nc.sync.dma_start(rotation_raw[:], rotation_rows[:, t, :])
            rotation_bf.append(held.tile([P, S], BF16, name=f"rotation_bf{t}"))
            for c in range(BANKS):
                cols = slice(c * BANK, (c + 1) * BANK)
                if last:
                    nc.sync.dma_start(rotation_raw[:, cols], rotation_rows[:, t, cols])
                if c % 2 == 0 or last:
                    nc.vector.tensor_copy(rotation_bf[t][:, cols], rotation_raw[:, cols])
                else:
                    nc.scalar.activation(rotation_bf[t][:, cols], rotation_raw[:, cols], COPY)

        offsets = held.tile([P, N // 16], U16, name="offsets")
        nc.sync.dma_start(offsets[:], offs)
        for first_tile in range(EARLY_TILES, D_TILES, LATE_TILES):
            load_and_centre_xt(1, 1, first_tile, LATE_TILES)
        for i in (2, 3):
            for first_tile in range(0, D_TILES, LATE_TILES):
                load_and_centre_xt(i, 1, first_tile, LATE_TILES)

        b1_w2 = held.tile([BLOCKS, K], F32, name="b1_w2")
        nc.gpsimd.tensor_tensor(b1_w2[:], b1_rows[:BLOCKS, :], w2_rows[:BLOCKS, 0:K], MULT)
        b1_share = held.tile([BLOCKS, 1], F32, name="b1_share")
        nc.scalar.activation(b1_w2[:], b1_w2[:], COPY, accum_out=b1_share[:])
        constant = held.tile([BLOCKS, 1], F32, name="constant")
        nc.gpsimd.tensor_tensor(constant[:], b1_share[:], b2_rows[:BLOCKS, :], ADD)

        age_term = held.tile([BLOCKS, P], F32, name="age_term")
        nc.gpsimd.tensor_scalar(age_term[:], age_rows[:], w2_rows[:BLOCKS, K : K + 1], constant[:], op0=MULT, op1=ADD)
        female_term = held.tile([BLOCKS, P], F32, name="female_term")
        nc.gpsimd.tensor_scalar(female_term[:], female_rows[:], w2_rows[:BLOCKS, K + 1 : K + 2], None, op0=MULT)
        covariates = held.tile([BLOCKS, P], F32, name="covariates")
        nc.gpsimd.tensor_tensor(covariates[:], age_term[:], female_term[:], ADD)

        sums = held.tile([P, BLOCKS, len(LAST_PIECES)], F32, name="sums")
        nc.vector.memset(sums[:], 0.0)

        p_tiles = []
        for i in range(BLOCKS):
            p_tiles.append(held.tile([P, S], F32, name=f"p{i}"))
            for c in range(BANKS):
                cols = slice(c * BANK, (c + 1) * BANK)
                bank = banks.tile([P, BANK], F32, tag="bank", name="bank")
                for t in range(D_TILES):
                    nc.tensor.matmul(
                        bank[:],
                        centred[i][t],
                        rotation_bf[t][:, cols],
                        start=(t == 0),
                        stop=(t == D_TILES - 1),
                    )
                if i == 0 and c == BANKS - 1:
                    nc.vector.tensor_copy(p_tiles[i][:, cols], bank[:])
                elif i == 0:
                    nc.scalar.activation(p_tiles[i][:, cols], bank[:], COPY)
                else:
                    placeholder = sums[:, i - 1, K - BANKS + c : K - BANKS + c + 1]
                    nc.scalar.activation(p_tiles[i][:, cols], bank[:], COPY, accum_out=placeholder)

        for i in range(BLOCKS):
            for column, (first, entries) in enumerate(LAST_PIECES if i == BLOCKS - 1 else PIECES):
                k = first // H
                product = products.tile([P, H], F32, name="product")
                nc.vector.tensor_tensor(
                    product[:, :entries],
                    p_tiles[i][:].indirect(offsets[:, first // 16 : (first + entries) // 16]),
                    w1_rows[:, first : first + entries],
                    MULT,
                )
                nc.scalar.activation(
                    product[:, :entries],
                    product[:, :entries],
                    COPY,
                    scale=w2_rows[:, k : k + 1],
                    accum_out=sums[:, i, column : column + 1],
                )

        score = held.tile([P, BLOCKS], F32, name="score")
        nc.vector.reduce_sum(score[:], sums[:], axis=mybir.AxisListType.X)

        score_t = banks.tile([P, BANK], F32, tag="bank", name="score_t")
        nc.tensor.transpose(score_t[:BLOCKS, :P], score[:], identity[:])
        result = held.tile([BLOCKS, P], F32, name="result")
        nc.vector.tensor_tensor(result[:], score_t[:BLOCKS, :P], covariates[:], ADD)
        nc.sync.dma_start(out.rearrange("(i p) one -> i (p one)", p=P), result[:])
